import numpy as np
import ml_dtypes


def mxq(x, axis, fmt="e4m3"):
    dtype, down = {"e4m3": (ml_dtypes.float8_e4m3fn, 7), "e5m2": (ml_dtypes.float8_e5m2, 14)}[fmt]
    v = np.moveaxis(np.asarray(x, np.float32).astype(ml_dtypes.bfloat16).astype(np.float64), axis, -1)
    blocks = v.reshape(v.shape[:-1] + (-1, 32))
    amax = np.abs(blocks).max(-1, keepdims=True)
    byte = np.maximum(np.where(amax > 0, np.frexp(amax)[1] - 1 + 127, 0) - down, 1)
    scale = np.exp2(byte - 127.0)
    codes = (blocks / scale).astype(np.float32).astype(dtype).astype(np.float64)
    return np.moveaxis((codes * scale).reshape(v.shape), -1, axis)


WIDE = False


def mx_kscale(k):
    if not WIDE:
        return np.ones(k)
    levels = np.array([10, -10, 5, -5, 0])
    a = np.random.permutation(np.resize(levels, k // 512 * 4)).reshape(k // 512, 4)
    idx = np.arange(k)
    return np.exp2(a[idx // 512, idx % 128 // 32])


BF16 = ml_dtypes.bfloat16


def bf(x):
    return np.asarray(x, np.float32).astype(BF16)


def f64(x):
    return np.asarray(x).astype(np.float64)


B, S, D_IN, D_OUT, R = 4, 256, 1024, 1024, 128
SCALING = 2.0


def setup_inputs():
    s = mx_kscale(D_IN)
    g = np.sqrt(np.mean(1.0 / (s * s)))
    return {"x": bf(np.random.standard_normal((B, S, D_IN)) * s),
            "weight": bf(np.random.standard_normal((D_OUT, D_IN)) / np.sqrt(D_IN) / s),
            "a_w": bf(np.random.standard_normal((R, D_IN)) / np.sqrt(D_IN) / s),
            "b_w": bf(np.random.standard_normal((D_OUT, R)) / np.sqrt(R)),
            "magnitude": bf((np.random.uniform(size=(1, D_OUT)) + 0.5) * g),
            "h_lora": bf(np.random.standard_normal((B, S, R)))}


def reference(x, weight, a_w, b_w, magnitude, h_lora):
    w = f64(weight)
    base_out = mxq(f64(x), 2, "e4m3") @ mxq(w, 1, "e4m3").T
    lora_out = SCALING * (f64(h_lora) @ f64(b_w).T)
    w_eff = w + SCALING * (f64(b_w) @ f64(a_w))
    weight_norm = np.sqrt((w_eff * w_eff).sum(axis=1))
    mag_norm_scale = (f64(magnitude) / weight_norm).reshape(1, 1, -1)
    dora_out = (mag_norm_scale - 1.0) * base_out + mag_norm_scale * lora_out
    return base_out + dora_out

@@ -1,0 +1,202 @@
+from contextlib import ExitStack
+
+import concourse.mybir as mybir
+from concourse.masks import make_identity
+
+F32 = mybir.dt.float32
+BF16 = mybir.dt.bfloat16
+U32 = mybir.dt.uint32
+U8 = mybir.dt.uint8
+FP8X4 = mybir.dt.float8_e4m3fn_x4
+ACT = mybir.ActivationFunctionType
+ALU = mybir.AluOpType
+
+P = 128
+PACK = 4
+BANK = 512
+
+TOKENS = 1024
+D_IN = 1024
+D_OUT = 1024
+RANK = 128
+SCALING = 2.0
+
+T_TILES = TOKENS // P
+O_TILES = D_OUT // P
+PASSES = D_IN // (P * PACK)
+HALVES = D_OUT // BANK
+O_TILES_PER_HALF = BANK // P
+WORD_BLOCKS = D_IN // 2 // P
+
+AHEAD = 2
+
+FLOPS = 2 * TOKENS * D_IN * D_OUT + 2 * TOKENS * RANK * D_OUT + 2 * D_OUT * RANK * D_IN
+
+
+def transpose_row_words(nc, bank, row_words, ident_f32):
+    for blk in range(WORD_BLOCKS):
+        nc.tensor.transpose(bank[:, blk, :], row_words[:, blk * P : (blk + 1) * P], ident_f32)
+
+
+def pairs_side_by_side(bank):
+    return bank[:].rearrange("p (g u) r -> p g r u", u=2)
+
+
+def tile_loralinear_pa_kernel(tc, x, weight, a_w, b_w, magnitude, h_lora, out):
+    nc = tc.nc
+    x_rows = x.flatten_outer_dims().rearrange("(p i) d -> p i d", i=T_TILES)
+    h_rows = h_lora.flatten_outer_dims().rearrange("(p i) r -> p i r", i=T_TILES)
+    out_rows = out.flatten_outer_dims().rearrange("(p i) o -> p i o", i=T_TILES)
+
+    with ExitStack() as ctx:
+        keep = ctx.enter_context(tc.tile_pool(name="keep", bufs=1))
+        work = ctx.enter_context(tc.tile_pool(name="work", bufs=3))
+        psum_turn = ctx.enter_context(tc.psum_pool(name="psum_turn", bufs=2))
+        psum_acc = ctx.enter_context(tc.psum_pool(name="psum_acc", bufs=6))
+
+        ident_bf16 = keep.tile([P, P], BF16)
+        make_identity(nc, ident_bf16[:])
+        ident_f32 = keep.tile([P, P], F32)
+        make_identity(nc, ident_f32[:])
+        table_warmer = keep.tile([P, 1], F32)
+        nc.vector.memset(table_warmer[:], 1.0)
+        nc.scalar.sqrt(table_warmer[:], table_warmer[:])
+        mag_rows = keep.tile([P, P], BF16)
+        nc.vector.memset(mag_rows[:], 0.0)
+
+        b_sb = keep.tile([P, O_TILES, RANK], BF16)
+        nc.sync.dma_start(out=b_sb[:], in_=b_w.rearrange("(j p) r -> p j r", p=P))
+        a_sb = keep.tile([P, D_IN], BF16)
+        nc.sync.dma_start(out=a_sb[:], in_=a_w)
+        w_sb = keep.tile([P, O_TILES, D_IN], BF16)
+        for j in range(O_TILES):
+            nc.sync.dma_start(out=w_sb[:, j, :], in_=weight[j * P : (j + 1) * P, :])
+        nc.sync.dma_start(
+            out=mag_rows[0:O_TILES, :], in_=magnitude.rearrange("one (j p) -> (one j) p", p=P)
+        )
+        h_sb = keep.tile([P, T_TILES, RANK], BF16)
+        nc.sync.dma_start(out=h_sb[:], in_=h_rows)
+        x_sb = keep.tile([P, T_TILES, D_IN], BF16)
+        for i in range(0, T_TILES, 2):
+            nc.sync.dma_start(out=x_sb[:, i : i + 2, :], in_=x_rows[:, i : i + 2, :])
+        w_words = w_sb[:].bitcast(F32)
+        x_words = x_sb[:].bitcast(F32)
+
+        b_turned = psum_turn.tile([P, O_TILES, P], BF16, tag="turn")
+        for j in range(O_TILES):
+            nc.tensor.transpose(b_turned[:, j, :], b_sb[:, j, :], ident_bf16[:])
+        b2T = keep.tile([P, D_OUT], BF16)
+        nc.scalar.mul(out=b2T[:], in_=b_turned[:].rearrange("r j o -> r (j o)"), mul=SCALING)
+
+        mag_turned = psum_turn.tile([P, P], BF16, tag="turn")
+        nc.tensor.transpose(mag_turned[:], mag_rows[:], ident_bf16[:])
+        mag_col = keep.tile([P, O_TILES], F32)
+        nc.vector.tensor_copy(out=mag_col[:], in_=mag_turned[:, 0:O_TILES])
+
+        w_grouped = keep.tile([P, HALVES, PASSES, BANK, PACK], BF16, align_bytes=64)
+        w_grouped_words = w_grouped[:].bitcast(F32)
+        w_codes = keep.tile([P, HALVES, PASSES, BANK], U32, align_bytes=64)
+        w_scales = keep.tile([P, HALVES, PASSES, BANK], U8, align_bytes=64)
+        norm_sq = keep.tile([P, O_TILES], F32)
+        for j in range(O_TILES):
+            half, j_in_half = divmod(j, O_TILES_PER_HALF)
+            w_turned = psum_turn.tile([P, WORD_BLOCKS, P], F32, tag="turn")
+            transpose_row_words(nc, w_turned, w_words[:, j, :], ident_f32[:])
+            nc.scalar.copy(
+                out=w_grouped_words[:, half, :, j_in_half * P : (j_in_half + 1) * P, :],
+                in_=pairs_side_by_side(w_turned),
+            )
+
+            w_eff = work.tile([P, D_IN], F32)
+            for c in range(D_IN // BANK):
+                cols = slice(c * BANK, (c + 1) * BANK)
+                ba2 = psum_acc.tile([P, BANK], F32, tag="acc")
+                nc.tensor.matmul(
+                    out=ba2[:], lhsT=b2T[:, j * P : (j + 1) * P], rhs=a_sb[:, cols],
+                    start=True, stop=True,
+                )
+                nc.vector.tensor_tensor(
+                    out=w_eff[:, cols], in0=ba2[:], in1=w_sb[:, j, cols], op=ALU.add
+                )
+            nc.scalar.activation(
+                out=w_eff[:], in_=w_eff[:], func=ACT.Square, accum_out=norm_sq[:, j : j + 1]
+            )
+
+            if j_in_half == O_TILES_PER_HALF - 1:
+                nc.vector.quantize_mx(
+                    out=w_codes[:, half, :, :].rearrange("p g o -> p (g o)").bitcast(FP8X4),
+                    scales=w_scales[:, half, :, :].rearrange("p g o -> p (g o)"),
+                    in_=w_grouped[:, half, :, :, :].rearrange("p g o t -> p (g o t)"),
+                )
+
+        norm = keep.tile([P, O_TILES], F32)
+        nc.scalar.sqrt(norm[:], norm_sq[:])
+        inv_norm = keep.tile([P, O_TILES], F32)
+        nc.vector.reciprocal(out=inv_norm[:], in_=norm[:])
+        m_col = keep.tile([P, O_TILES], F32)
+        nc.vector.tensor_tensor(out=m_col[:], in0=inv_norm[:], in1=mag_col[:], op=ALU.mult)
+        m_all = keep.tile([P, D_OUT], F32)
+        for half in range(HALVES):
+            m_turned = psum_turn.tile([P, O_TILES_PER_HALF, P], F32, tag="turn")
+            for j_in_half in range(O_TILES_PER_HALF):
+                j = half * O_TILES_PER_HALF + j_in_half
+                nc.tensor.transpose(
+                    m_turned[:, j_in_half, :], m_col[:, j : j + 1].to_broadcast([P, P]), ident_f32[:]
+                )
+            nc.scalar.copy(
+                out=m_all[:, half * BANK : (half + 1) * BANK],
+                in_=m_turned[:].rearrange("p j o -> p (j o)"),
+            )
+
+        h_turned = psum_turn.tile([P, T_TILES, P], BF16, tag="turn")
+        for i in range(T_TILES):
+            nc.tensor.transpose(h_turned[:, i, :], h_sb[:, i, :], ident_bf16[:])
+        hT = keep.tile([P, T_TILES, P], BF16)
+        nc.scalar.copy(out=hT[:], in_=h_turned[:])
+
+        x_grouped = keep.tile([P, T_TILES, PASSES, P, PACK], BF16, align_bytes=64)
+        x_grouped_words = x_grouped[:].bitcast(F32)
+        x_codes = keep.tile([P, T_TILES, PASSES, P], U32, align_bytes=64)
+        x_scales = keep.tile([P, T_TILES, PASSES, P], U8, align_bytes=64)
+
+        def quantise_tokens(i):
+            x_turned = psum_turn.tile([P, WORD_BLOCKS, P], F32, tag="turn")
+            transpose_row_words(nc, x_turned, x_words[:, i, :], ident_f32[:])
+            nc.scalar.copy(out=x_grouped_words[:, i, :, :, :], in_=pairs_side_by_side(x_turned))
+            nc.vector.quantize_mx(
+                out=x_codes[:, i, :, :].rearrange("p g r -> p (g r)").bitcast(FP8X4),
+                scales=x_scales[:, i, :, :].rearrange("p g r -> p (g r)"),
+                in_=x_grouped[:, i, :, :, :].rearrange("p g r t -> p (g r t)"),
+            )
+
+        def finish_tokens(i):
+            result = work.tile([P, D_OUT], F32)
+            for half in range(HALVES):
+                cols = slice(half * BANK, (half + 1) * BANK)
+                lora = psum_acc.tile([P, BANK], F32, tag="acc")
+                nc.tensor.matmul(
+                    out=lora[:], lhsT=hT[:, i, :], rhs=b2T[:, cols], start=True, stop=True
+                )
+                nc.scalar.copy(out=result[:, cols], in_=lora[:])
+                base = psum_acc.tile([P, BANK], F32, tag="acc")
+                for g in range(PASSES):
+                    nc.tensor.matmul_mx(
+                        out=base[:],
+                        lhsT=x_codes[:, i, g, :].bitcast(FP8X4),
+                        lhsT_scale=x_scales[:, i, g, :],
+                        rhs=w_codes[:, half, g, :].bitcast(FP8X4),
+                        rhs_scale=w_scales[:, half, g, :],
+                        start=(g == 0),
+                        stop=(g == PASSES - 1),
+                    )
+                nc.vector.tensor_tensor(
+                    out=result[:, cols], in0=base[:], in1=result[:, cols], op=ALU.add
+                )
+            nc.vector.tensor_tensor(out=result[:], in0=result[:], in1=m_all[:], op=ALU.mult)
+            nc.sync.dma_start(out=out_rows[:, i, :], in_=result[:])
+
+        for i in range(T_TILES + AHEAD):
+            if i < T_TILES:
+                quantise_tokens(i)
+            if i >= AHEAD:
+                finish_tokens(i - AHEAD)

@@ -28,18 +28,11 @@ HALVES = D_OUT // BANK
 O_TILES_PER_HALF = BANK // P
 WORD_BLOCKS = D_IN // 2 // P
 
-AHEAD = 2
+EARLY = 2
+SCALE_LAG = 2
+SCALAR_W_BANKS = 4
 
 FLOPS = 2 * TOKENS * D_IN * D_OUT + 2 * TOKENS * RANK * D_OUT + 2 * D_OUT * RANK * D_IN
-
-
-def transpose_row_words(nc, bank, row_words, ident_f32):
-    for blk in range(WORD_BLOCKS):
-        nc.tensor.transpose(bank[:, blk, :], row_words[:, blk * P : (blk + 1) * P], ident_f32)
-
-
-def pairs_side_by_side(bank):
-    return bank[:].rearrange("p (g u) r -> p g r u", u=2)
 
 
 def tile_loralinear_pa_kernel(tc, x, weight, a_w, b_w, magnitude, h_lora, out):
@@ -50,9 +43,10 @@ def tile_loralinear_pa_kernel(tc, x, weight, a_w, b_w, magnitude, h_lora, out):
 
     with ExitStack() as ctx:
         keep = ctx.enter_context(tc.tile_pool(name="keep", bufs=1))
-        work = ctx.enter_context(tc.tile_pool(name="work", bufs=3))
-        psum_turn = ctx.enter_context(tc.psum_pool(name="psum_turn", bufs=2))
-        psum_acc = ctx.enter_context(tc.psum_pool(name="psum_acc", bufs=6))
+        merged = ctx.enter_context(tc.tile_pool(name="merged", bufs=4))
+        psum_turn = ctx.enter_context(tc.psum_pool(name="psum_turn", bufs=3))
+        psum_acc = ctx.enter_context(tc.psum_pool(name="psum_acc", bufs=5))
+        ctx.enter_context(tc.manual_schedule())
 
         ident_bf16 = keep.tile([P, P], BF16)
         make_identity(nc, ident_bf16[:])
@@ -71,113 +65,100 @@ def tile_loralinear_pa_kernel(tc, x, weight, a_w, b_w, magnitude, h_lora, out):
         w_sb = keep.tile([P, O_TILES, D_IN], BF16)
         for j in range(O_TILES):
             nc.sync.dma_start(out=w_sb[:, j, :], in_=weight[j * P : (j + 1) * P, :])
-        nc.sync.dma_start(
-            out=mag_rows[0:O_TILES, :], in_=magnitude.rearrange("one (j p) -> (one j) p", p=P)
-        )
         h_sb = keep.tile([P, T_TILES, RANK], BF16)
         nc.sync.dma_start(out=h_sb[:], in_=h_rows)
         x_sb = keep.tile([P, T_TILES, D_IN], BF16)
         for i in range(0, T_TILES, 2):
             nc.sync.dma_start(out=x_sb[:, i : i + 2, :], in_=x_rows[:, i : i + 2, :])
+        nc.sync.dma_start(
+            out=mag_rows[0:O_TILES, :], in_=magnitude.rearrange("one (j p) -> (one j) p", p=P)
+        )
         w_words = w_sb[:].bitcast(F32)
         x_words = x_sb[:].bitcast(F32)
 
-        b_turned = psum_turn.tile([P, O_TILES, P], BF16, tag="turn")
-        for j in range(O_TILES):
-            nc.tensor.transpose(b_turned[:, j, :], b_sb[:, j, :], ident_bf16[:])
         b2T = keep.tile([P, D_OUT], BF16)
-        nc.scalar.mul(out=b2T[:], in_=b_turned[:].rearrange("r j o -> r (j o)"), mul=SCALING)
-
-        mag_turned = psum_turn.tile([P, P], BF16, tag="turn")
-        nc.tensor.transpose(mag_turned[:], mag_rows[:], ident_bf16[:])
-        mag_col = keep.tile([P, O_TILES], F32)
-        nc.vector.tensor_copy(out=mag_col[:], in_=mag_turned[:, 0:O_TILES])
-
+        hT = keep.tile([P, T_TILES, P], BF16)
         w_grouped = keep.tile([P, HALVES, PASSES, BANK, PACK], BF16, align_bytes=64)
         w_grouped_words = w_grouped[:].bitcast(F32)
         w_codes = keep.tile([P, HALVES, PASSES, BANK], U32, align_bytes=64)
         w_scales = keep.tile([P, HALVES, PASSES, BANK], U8, align_bytes=64)
-        norm_sq = keep.tile([P, O_TILES], F32)
-        for j in range(O_TILES):
-            half, j_in_half = divmod(j, O_TILES_PER_HALF)
-            w_turned = psum_turn.tile([P, WORD_BLOCKS, P], F32, tag="turn")
-            transpose_row_words(nc, w_turned, w_words[:, j, :], ident_f32[:])
-            nc.scalar.copy(
-                out=w_grouped_words[:, half, :, j_in_half * P : (j_in_half + 1) * P, :],
-                in_=pairs_side_by_side(w_turned),
-            )
-
-            w_eff = work.tile([P, D_IN], F32)
-            for c in range(D_IN // BANK):
-                cols = slice(c * BANK, (c + 1) * BANK)
-                ba2 = psum_acc.tile([P, BANK], F32, tag="acc")
-                nc.tensor.matmul(
-                    out=ba2[:], lhsT=b2T[:, j * P : (j + 1) * P], rhs=a_sb[:, cols],
-                    start=True, stop=True,
-                )
-                nc.vector.tensor_tensor(
-                    out=w_eff[:, cols], in0=ba2[:], in1=w_sb[:, j, cols], op=ALU.add
-                )
-            nc.scalar.activation(
-                out=w_eff[:], in_=w_eff[:], func=ACT.Square, accum_out=norm_sq[:, j : j + 1]
-            )
-
-            if j_in_half == O_TILES_PER_HALF - 1:
-                nc.vector.quantize_mx(
-                    out=w_codes[:, half, :, :].rearrange("p g o -> p (g o)").bitcast(FP8X4),
-                    scales=w_scales[:, half, :, :].rearrange("p g o -> p (g o)"),
-                    in_=w_grouped[:, half, :, :, :].rearrange("p g o t -> p (g o t)"),
-                )
-
-        norm = keep.tile([P, O_TILES], F32)
-        nc.scalar.sqrt(norm[:], norm_sq[:])
-        inv_norm = keep.tile([P, O_TILES], F32)
-        nc.vector.reciprocal(out=inv_norm[:], in_=norm[:])
-        m_col = keep.tile([P, O_TILES], F32)
-        nc.vector.tensor_tensor(out=m_col[:], in0=inv_norm[:], in1=mag_col[:], op=ALU.mult)
-        m_all = keep.tile([P, D_OUT], F32)
-        for half in range(HALVES):
-            m_turned = psum_turn.tile([P, O_TILES_PER_HALF, P], F32, tag="turn")
-            for j_in_half in range(O_TILES_PER_HALF):
-                j = half * O_TILES_PER_HALF + j_in_half
-                nc.tensor.transpose(
-                    m_turned[:, j_in_half, :], m_col[:, j : j + 1].to_broadcast([P, P]), ident_f32[:]
-                )
-            nc.scalar.copy(
-                out=m_all[:, half * BANK : (half + 1) * BANK],
-                in_=m_turned[:].rearrange("p j o -> p (j o)"),
-            )
-
-        h_turned = psum_turn.tile([P, T_TILES, P], BF16, tag="turn")
-        for i in range(T_TILES):
-            nc.tensor.transpose(h_turned[:, i, :], h_sb[:, i, :], ident_bf16[:])
-        hT = keep.tile([P, T_TILES, P], BF16)
-        nc.scalar.copy(out=hT[:], in_=h_turned[:])
-
         x_grouped = keep.tile([P, T_TILES, PASSES, P, PACK], BF16, align_bytes=64)
         x_grouped_words = x_grouped[:].bitcast(F32)
         x_codes = keep.tile([P, T_TILES, PASSES, P], U32, align_bytes=64)
         x_scales = keep.tile([P, T_TILES, PASSES, P], U8, align_bytes=64)
+        norm_sq = keep.tile([P, O_TILES], F32)
+        m_all = keep.tile([P, D_OUT], F32)
+        results = keep.tile([P, T_TILES, D_OUT], F32)
+
+        def turn_words(row_words):
+            bank = psum_turn.tile([P, WORD_BLOCKS, P], F32, tag="turn")
+            for blk in range(WORD_BLOCKS):
+                nc.tensor.transpose(
+                    bank[:, blk, :], row_words[:, blk * P : (blk + 1) * P], ident_f32[:]
+                )
+            return bank
+
+        def group_words(on_vector, grouped_words, bank):
+            side_by_side = bank[:].rearrange("p (g u) r -> p g r u", u=2)
+            if on_vector:
+                nc.vector.tensor_copy(out=grouped_words, in_=side_by_side)
+            else:
+                nc.scalar.copy(out=grouped_words, in_=side_by_side)
+
+        def group_weight_words(j, bank):
+            half, j_in_half = divmod(j, O_TILES_PER_HALF)
+            group_words(
+                j >= SCALAR_W_BANKS,
+                w_grouped_words[:, half, :, j_in_half * P : (j_in_half + 1) * P, :],
+                bank,
+            )
+
+        def quantise_weight(half):
+            nc.vector.quantize_mx(
+                out=w_codes[:, half, :, :].rearrange("p g o -> p (g o)").bitcast(FP8X4),
+                scales=w_scales[:, half, :, :].rearrange("p g o -> p (g o)"),
+                in_=w_grouped[:, half, :, :, :].rearrange("p g o t -> p (g o t)"),
+            )
 
         def quantise_tokens(i):
-            x_turned = psum_turn.tile([P, WORD_BLOCKS, P], F32, tag="turn")
-            transpose_row_words(nc, x_turned, x_words[:, i, :], ident_f32[:])
-            nc.scalar.copy(out=x_grouped_words[:, i, :, :, :], in_=pairs_side_by_side(x_turned))
             nc.vector.quantize_mx(
                 out=x_codes[:, i, :, :].rearrange("p g r -> p (g r)").bitcast(FP8X4),
                 scales=x_scales[:, i, :, :].rearrange("p g r -> p (g r)"),
                 in_=x_grouped[:, i, :, :, :].rearrange("p g r t -> p (g r t)"),
             )
 
-        def finish_tokens(i):
-            result = work.tile([P, D_OUT], F32)
+        def adapter_weight_products(j):
+            banks = []
+            for c in range(D_IN // BANK):
+                ba2 = psum_acc.tile([P, BANK], F32, tag="acc", name="ba2")
+                nc.tensor.matmul(
+                    out=ba2[:], lhsT=b2T[:, j * P : (j + 1) * P],
+                    rhs=a_sb[:, c * BANK : (c + 1) * BANK], start=True, stop=True,
+                )
+                banks.append(ba2)
+            return banks
+
+        def merge_weight(j, banks):
+            w_eff = merged.tile([P, D_IN], F32)
+            for c in range(D_IN // BANK):
+                cols = slice(c * BANK, (c + 1) * BANK)
+                nc.vector.tensor_tensor(
+                    out=w_eff[:, cols], in0=banks[c][:], in1=w_sb[:, j, cols], op=ALU.add
+                )
+            return w_eff
+
+        def lora_products(i):
             for half in range(HALVES):
                 cols = slice(half * BANK, (half + 1) * BANK)
                 lora = psum_acc.tile([P, BANK], F32, tag="acc")
                 nc.tensor.matmul(
                     out=lora[:], lhsT=hT[:, i, :], rhs=b2T[:, cols], start=True, stop=True
                 )
-                nc.scalar.copy(out=result[:, cols], in_=lora[:])
+                nc.scalar.copy(out=results[:, i, cols], in_=lora[:])
+
+        def add_base_products(i):
+            for half in range(HALVES):
+                cols = slice(half * BANK, (half + 1) * BANK)
                 base = psum_acc.tile([P, BANK], F32, tag="acc")
                 for g in range(PASSES):
                     nc.tensor.matmul_mx(
@@ -190,13 +171,89 @@ def tile_loralinear_pa_kernel(tc, x, weight, a_w, b_w, magnitude, h_lora, out):
                         stop=(g == PASSES - 1),
                     )
                 nc.vector.tensor_tensor(
-                    out=result[:, cols], in0=base[:], in1=result[:, cols], op=ALU.add
+                    out=results[:, i, cols], in0=base[:], in1=results[:, i, cols], op=ALU.add
                 )
-            nc.vector.tensor_tensor(out=result[:], in0=result[:], in1=m_all[:], op=ALU.mult)
-            nc.sync.dma_start(out=out_rows[:, i, :], in_=result[:])
 
-        for i in range(T_TILES + AHEAD):
+        def scale_and_store(i):
+            nc.vector.tensor_tensor(
+                out=results[:, i, 0:BANK], in0=results[:, i, 0:BANK], in1=m_all[:, 0:BANK],
+                op=ALU.mult,
+            )
+            nc.gpsimd.tensor_tensor(
+                out=results[:, i, BANK:D_OUT], in0=results[:, i, BANK:D_OUT],
+                in1=m_all[:, BANK:D_OUT], op=ALU.mult,
+            )
+            nc.sync.dma_start(out=out_rows[:, i, :], in_=results[:, i, :])
+
+        b_turned = psum_turn.tile([P, O_TILES, P], BF16, tag="turn")
+        for j in range(O_TILES):
+            nc.tensor.transpose(b_turned[:, j, :], b_sb[:, j, :], ident_bf16[:])
+        nc.scalar.mul(out=b2T[:], in_=b_turned[:].rearrange("r j o -> r (j o)"), mul=SCALING)
+
+        group_weight_words(0, turn_words(w_words[:, 0, :]))
+        for j in range(O_TILES):
+            ba2_banks = adapter_weight_products(j)
+            if j + 1 < O_TILES:
+                w_turned = turn_words(w_words[:, j + 1, :])
+            w_eff = merge_weight(j, ba2_banks)
+            if j + 1 < O_TILES:
+                group_weight_words(j + 1, w_turned)
+            if j == O_TILES - 1 - EARLY:
+                h_turned = psum_turn.tile([P, T_TILES, P], BF16, tag="turn")
+                for i in range(T_TILES):
+                    nc.tensor.transpose(h_turned[:, i, :], h_sb[:, i, :], ident_bf16[:])
+                nc.scalar.copy(out=hT[:], in_=h_turned[:])
+            if j >= O_TILES - EARLY:
+                i = j - (O_TILES - EARLY)
+                group_words(False, x_grouped_words[:, i, :, :, :], turn_words(x_words[:, i, :]))
+            nc.scalar.activation(
+                out=w_eff[:], in_=w_eff[:], func=ACT.Square, accum_out=norm_sq[:, j : j + 1]
+            )
+            if j == O_TILES_PER_HALF:
+                quantise_weight(0)
+
+        mag_turned = psum_turn.tile([P, P], BF16, tag="turn")
+        nc.tensor.transpose(mag_turned[:], mag_rows[:], ident_bf16[:])
+        mag_col = keep.tile([P, O_TILES], F32)
+        nc.vector.tensor_copy(out=mag_col[:], in_=mag_turned[:, 0:O_TILES])
+
+        quantise_tokens(0)
+        quantise_weight(1)
+        for i in range(1, EARLY):
+            quantise_tokens(i)
+        norm = keep.tile([P, O_TILES], F32)
+        nc.scalar.sqrt(norm[:], norm_sq[:])
+
+        for i in range(T_TILES + SCALE_LAG):
             if i < T_TILES:
-                quantise_tokens(i)
-            if i >= AHEAD:
-                finish_tokens(i - AHEAD)
+                lora_products(i)
+                if i + EARLY < T_TILES:
+                    group_words(
+                        False,
+                        x_grouped_words[:, i + EARLY, :, :, :],
+                        turn_words(x_words[:, i + EARLY, :]),
+                    )
+                add_base_products(i)
+                if i + EARLY < T_TILES:
+                    quantise_tokens(i + EARLY)
+            if i == 0:
+                inv_norm = keep.tile([P, O_TILES], F32)
+                nc.vector.reciprocal(out=inv_norm[:], in_=norm[:])
+                m_col = keep.tile([P, O_TILES], F32)
+                nc.vector.tensor_tensor(out=m_col[:], in0=inv_norm[:], in1=mag_col[:], op=ALU.mult)
+            if i == 1:
+                for half in range(HALVES):
+                    m_turned = psum_turn.tile([P, O_TILES_PER_HALF, P], F32, tag="turn")
+                    for j_in_half in range(O_TILES_PER_HALF):
+                        j = half * O_TILES_PER_HALF + j_in_half
+                        nc.tensor.transpose(
+                            m_turned[:, j_in_half, :],
+                            m_col[:, j : j + 1].to_broadcast([P, P]),
+                            ident_f32[:],
+                        )
+                    nc.scalar.copy(
+                        out=m_all[:, half * BANK : (half + 1) * BANK],
+                        in_=m_turned[:].rearrange("p j o -> p (j o)"),
+                    )
+            if i >= SCALE_LAG:
+                scale_and_store(i - SCALE_LAG)

@@ -29,8 +29,9 @@ O_TILES_PER_HALF = BANK // P
 WORD_BLOCKS = D_IN // 2 // P
 
 EARLY = 2
-SCALE_LAG = 2
+SCALE_LAG = 1
 SCALAR_W_BANKS = 4
+VECTOR_COLUMNS = 384
 
 FLOPS = 2 * TOKENS * D_IN * D_OUT + 2 * TOKENS * RANK * D_OUT + 2 * D_OUT * RANK * D_IN
 
@@ -175,29 +176,35 @@ def tile_loralinear_pa_kernel(tc, x, weight, a_w, b_w, magnitude, h_lora, out):
                 )
 
         def scale_and_store(i):
-            nc.vector.tensor_tensor(
-                out=results[:, i, 0:BANK], in0=results[:, i, 0:BANK], in1=m_all[:, 0:BANK],
-                op=ALU.mult,
-            )
-            nc.gpsimd.tensor_tensor(
-                out=results[:, i, BANK:D_OUT], in0=results[:, i, BANK:D_OUT],
-                in1=m_all[:, BANK:D_OUT], op=ALU.mult,
-            )
-            nc.sync.dma_start(out=out_rows[:, i, :], in_=results[:, i, :])
+            for engine, cols in (
+                (nc.vector, slice(0, VECTOR_COLUMNS)),
+                (nc.gpsimd, slice(VECTOR_COLUMNS, D_OUT)),
+            ):
+                engine.tensor_tensor(
+                    out=results[:, i, cols], in0=results[:, i, cols], in1=m_all[:, cols],
+                    op=ALU.mult,
+                )
+                nc.sync.dma_start(out=out_rows[:, i, cols], in_=results[:, i, cols])
 
-        b_turned = psum_turn.tile([P, O_TILES, P], BF16, tag="turn")
-        for j in range(O_TILES):
-            nc.tensor.transpose(b_turned[:, j, :], b_sb[:, j, :], ident_bf16[:])
-        nc.scalar.mul(out=b2T[:], in_=b_turned[:].rearrange("r j o -> r (j o)"), mul=SCALING)
+        for half in range(HALVES):
+            b_turned = psum_turn.tile([P, O_TILES_PER_HALF, P], BF16, tag="turn")
+            for j_in_half in range(O_TILES_PER_HALF):
+                nc.tensor.transpose(
+                    b_turned[:, j_in_half, :],
+                    b_sb[:, half * O_TILES_PER_HALF + j_in_half, :],
+                    ident_bf16[:],
+                )
+            nc.scalar.mul(
+                out=b2T[:, half * BANK : (half + 1) * BANK],
+                in_=b_turned[:].rearrange("r j o -> r (j o)"),
+                mul=SCALING,
+            )
 
-        group_weight_words(0, turn_words(w_words[:, 0, :]))
         for j in range(O_TILES):
             ba2_banks = adapter_weight_products(j)
-            if j + 1 < O_TILES:
-                w_turned = turn_words(w_words[:, j + 1, :])
+            w_turned = turn_words(w_words[:, j, :])
             w_eff = merge_weight(j, ba2_banks)
-            if j + 1 < O_TILES:
-                group_weight_words(j + 1, w_turned)
+            group_weight_words(j, w_turned)
             if j == O_TILES - 1 - EARLY:
                 h_turned = psum_turn.tile([P, T_TILES, P], BF16, tag="turn")
                 for i in range(T_TILES):

@@ -30,10 +30,14 @@ WORD_BLOCKS = D_IN // 2 // P
 
 EARLY = 2
 SCALE_LAG = 1
-SCALAR_W_BANKS = 4
-VECTOR_COLUMNS = 384
+SCALAR_W_BANKS = 2
+TILES_MERGED_ON_TENSOR = 3
 
 FLOPS = 2 * TOKENS * D_IN * D_OUT + 2 * TOKENS * RANK * D_OUT + 2 * D_OUT * RANK * D_IN
+
+
+def merged_on_tensor(j):
+    return O_TILES - 1 - TILES_MERGED_ON_TENSOR <= j < O_TILES - 1
 
 
 def tile_loralinear_pa_kernel(tc, x, weight, a_w, b_w, magnitude, h_lora, out):
@@ -45,8 +49,8 @@ def tile_loralinear_pa_kernel(tc, x, weight, a_w, b_w, magnitude, h_lora, out):
     with ExitStack() as ctx:
         keep = ctx.enter_context(tc.tile_pool(name="keep", bufs=1))
         merged = ctx.enter_context(tc.tile_pool(name="merged", bufs=4))
-        psum_turn = ctx.enter_context(tc.psum_pool(name="psum_turn", bufs=3))
-        psum_acc = ctx.enter_context(tc.psum_pool(name="psum_acc", bufs=5))
+        psum = ctx.enter_context(tc.psum_pool(name="psum", bufs=7))
+        psum_kept = ctx.enter_context(tc.psum_pool(name="psum_kept", bufs=1))
         ctx.enter_context(tc.manual_schedule())
 
         ident_bf16 = keep.tile([P, P], BF16)
@@ -87,12 +91,14 @@ def tile_loralinear_pa_kernel(tc, x, weight, a_w, b_w, magnitude, h_lora, out):
         x_grouped_words = x_grouped[:].bitcast(F32)
         x_codes = keep.tile([P, T_TILES, PASSES, P], U32, align_bytes=64)
         x_scales = keep.tile([P, T_TILES, PASSES, P], U8, align_bytes=64)
-        norm_sq = keep.tile([P, O_TILES], F32)
-        m_all = keep.tile([P, D_OUT], F32)
+        norm_sq_parts = keep.tile([P, D_IN // BANK, O_TILES], F32)
+        nc.vector.memset(norm_sq_parts[:], 0.0)
+        m_first = keep.tile([P, BANK], F32)
+        m_second = psum_kept.tile([P, O_TILES_PER_HALF, P], F32)
         results = keep.tile([P, T_TILES, D_OUT], F32)
 
         def turn_words(row_words):
-            bank = psum_turn.tile([P, WORD_BLOCKS, P], F32, tag="turn")
+            bank = psum.tile([P, WORD_BLOCKS, P], F32, tag="bank")
             for blk in range(WORD_BLOCKS):
                 nc.tensor.transpose(
                     bank[:, blk, :], row_words[:, blk * P : (blk + 1) * P], ident_f32[:]
@@ -131,27 +137,43 @@ def tile_loralinear_pa_kernel(tc, x, weight, a_w, b_w, magnitude, h_lora, out):
         def adapter_weight_products(j):
             banks = []
             for c in range(D_IN // BANK):
-                ba2 = psum_acc.tile([P, BANK], F32, tag="acc", name="ba2")
+                cols = slice(c * BANK, (c + 1) * BANK)
+                ba2 = psum.tile([P, BANK], F32, tag="bank", name="ba2")
+                if merged_on_tensor(j):
+                    nc.tensor.matmul(
+                        out=ba2[:], lhsT=ident_bf16[:], rhs=w_sb[:, j, cols], start=True, stop=False
+                    )
                 nc.tensor.matmul(
-                    out=ba2[:], lhsT=b2T[:, j * P : (j + 1) * P],
-                    rhs=a_sb[:, c * BANK : (c + 1) * BANK], start=True, stop=True,
+                    out=ba2[:], lhsT=b2T[:, j * P : (j + 1) * P], rhs=a_sb[:, cols],
+                    start=(not merged_on_tensor(j)), stop=True,
                 )
                 banks.append(ba2)
             return banks
 
-        def merge_weight(j, banks):
-            w_eff = merged.tile([P, D_IN], F32)
+        def merge_weight(j, banks, w_eff):
             for c in range(D_IN // BANK):
                 cols = slice(c * BANK, (c + 1) * BANK)
                 nc.vector.tensor_tensor(
                     out=w_eff[:, cols], in0=banks[c][:], in1=w_sb[:, j, cols], op=ALU.add
                 )
-            return w_eff
+
+        def sum_squares(j, banks, w_eff):
+            if merged_on_tensor(j):
+                for c in range(D_IN // BANK):
+                    nc.scalar.activation(
+                        out=w_eff[:, c * BANK : (c + 1) * BANK], in_=banks[c][:], func=ACT.Square,
+                        accum_out=norm_sq_parts[:, c, j : j + 1],
+                    )
+            else:
+                nc.scalar.activation(
+                    out=w_eff[:], in_=w_eff[:], func=ACT.Square,
+                    accum_out=norm_sq_parts[:, 0, j : j + 1],
+                )
 
         def lora_products(i):
             for half in range(HALVES):
                 cols = slice(half * BANK, (half + 1) * BANK)
-                lora = psum_acc.tile([P, BANK], F32, tag="acc")
+                lora = psum.tile([P, BANK], F32, tag="bank")
                 nc.tensor.matmul(
                     out=lora[:], lhsT=hT[:, i, :], rhs=b2T[:, cols], start=True, stop=True
                 )
@@ -160,7 +182,7 @@ def tile_loralinear_pa_kernel(tc, x, weight, a_w, b_w, magnitude, h_lora, out):
         def add_base_products(i):
             for half in range(HALVES):
                 cols = slice(half * BANK, (half + 1) * BANK)
-                base = psum_acc.tile([P, BANK], F32, tag="acc")
+                base = psum.tile([P, BANK], F32, tag="bank")
                 for g in range(PASSES):
                     nc.tensor.matmul_mx(
                         out=base[:],
@@ -176,18 +198,20 @@ def tile_loralinear_pa_kernel(tc, x, weight, a_w, b_w, magnitude, h_lora, out):
                 )
 
         def scale_and_store(i):
-            for engine, cols in (
-                (nc.vector, slice(0, VECTOR_COLUMNS)),
-                (nc.gpsimd, slice(VECTOR_COLUMNS, D_OUT)),
-            ):
-                engine.tensor_tensor(
-                    out=results[:, i, cols], in0=results[:, i, cols], in1=m_all[:, cols],
-                    op=ALU.mult,
-                )
-                nc.sync.dma_start(out=out_rows[:, i, cols], in_=results[:, i, cols])
+            nc.gpsimd.tensor_tensor(
+                out=results[:, i, 0:BANK], in0=results[:, i, 0:BANK], in1=m_first[:], op=ALU.mult
+            )
+            nc.sync.dma_start(out=out_rows[:, i, 0:BANK], in_=results[:, i, 0:BANK])
+            nc.vector.tensor_tensor(
+                out=results[:, i, BANK:D_OUT],
+                in0=m_second[:].rearrange("p j o -> p (j o)"),
+                in1=results[:, i, BANK:D_OUT],
+                op=ALU.mult,
+            )
+            nc.sync.dma_start(out=out_rows[:, i, BANK:D_OUT], in_=results[:, i, BANK:D_OUT])
 
         for half in range(HALVES):
-            b_turned = psum_turn.tile([P, O_TILES_PER_HALF, P], BF16, tag="turn")
+            b_turned = psum.tile([P, O_TILES_PER_HALF, P], BF16, tag="bank")
             for j_in_half in range(O_TILES_PER_HALF):
                 nc.tensor.transpose(
                     b_turned[:, j_in_half, :],
@@ -203,23 +227,23 @@ def tile_loralinear_pa_kernel(tc, x, weight, a_w, b_w, magnitude, h_lora, out):
         for j in range(O_TILES):
             ba2_banks = adapter_weight_products(j)
             w_turned = turn_words(w_words[:, j, :])
-            w_eff = merge_weight(j, ba2_banks)
+            w_eff = merged.tile([P, D_IN], F32)
+            if not merged_on_tensor(j):
+                merge_weight(j, ba2_banks, w_eff)
             group_weight_words(j, w_turned)
             if j == O_TILES - 1 - EARLY:
-                h_turned = psum_turn.tile([P, T_TILES, P], BF16, tag="turn")
+                h_turned = psum.tile([P, T_TILES, P], BF16, tag="bank")
                 for i in range(T_TILES):
                     nc.tensor.transpose(h_turned[:, i, :], h_sb[:, i, :], ident_bf16[:])
                 nc.scalar.copy(out=hT[:], in_=h_turned[:])
             if j >= O_TILES - EARLY:
                 i = j - (O_TILES - EARLY)
                 group_words(False, x_grouped_words[:, i, :, :, :], turn_words(x_words[:, i, :]))
-            nc.scalar.activation(
-                out=w_eff[:], in_=w_eff[:], func=ACT.Square, accum_out=norm_sq[:, j : j + 1]
-            )
+            sum_squares(j, ba2_banks, w_eff)
             if j == O_TILES_PER_HALF:
                 quantise_weight(0)
 
-        mag_turned = psum_turn.tile([P, P], BF16, tag="turn")
+        mag_turned = psum.tile([P, P], BF16, tag="bank")
         nc.tensor.transpose(mag_turned[:], mag_rows[:], ident_bf16[:])
         mag_col = keep.tile([P, O_TILES], F32)
         nc.vector.tensor_copy(out=mag_col[:], in_=mag_turned[:, 0:O_TILES])
@@ -228,12 +252,17 @@ def tile_loralinear_pa_kernel(tc, x, weight, a_w, b_w, magnitude, h_lora, out):
         quantise_weight(1)
         for i in range(1, EARLY):
             quantise_tokens(i)
+        norm_sq = keep.tile([P, O_TILES], F32)
+        nc.vector.tensor_tensor(
+            out=norm_sq[:], in0=norm_sq_parts[:, 0, :], in1=norm_sq_parts[:, 1, :], op=ALU.add
+        )
         norm = keep.tile([P, O_TILES], F32)
-        nc.scalar.sqrt(norm[:], norm_sq[:])
 
         for i in range(T_TILES + SCALE_LAG):
             if i < T_TILES:
                 lora_products(i)
+                if i == 0:
+                    nc.scalar.sqrt(norm[:], norm_sq[:])
                 if i + EARLY < T_TILES:
                     group_words(
                         False,
@@ -249,18 +278,14 @@ def tile_loralinear_pa_kernel(tc, x, weight, a_w, b_w, magnitude, h_lora, out):
                 m_col = keep.tile([P, O_TILES], F32)
                 nc.vector.tensor_tensor(out=m_col[:], in0=inv_norm[:], in1=mag_col[:], op=ALU.mult)
             if i == 1:
-                for half in range(HALVES):
-                    m_turned = psum_turn.tile([P, O_TILES_PER_HALF, P], F32, tag="turn")
-                    for j_in_half in range(O_TILES_PER_HALF):
-                        j = half * O_TILES_PER_HALF + j_in_half
-                        nc.tensor.transpose(
-                            m_turned[:, j_in_half, :],
-                            m_col[:, j : j + 1].to_broadcast([P, P]),
-                            ident_f32[:],
-                        )
-                    nc.scalar.copy(
-                        out=m_all[:, half * BANK : (half + 1) * BANK],
-                        in_=m_turned[:].rearrange("p j o -> p (j o)"),
+                m_turned = psum.tile([P, O_TILES_PER_HALF, P], F32, tag="bank")
+                for j in range(O_TILES):
+                    half, j_in_half = divmod(j, O_TILES_PER_HALF)
+                    nc.tensor.transpose(
+                        (m_turned, m_second)[half][:, j_in_half, :],
+                        m_col[:, j : j + 1].to_broadcast([P, P]),
+                        ident_f32[:],
                     )
+                nc.scalar.copy(out=m_first[:], in_=m_turned[:].rearrange("p j o -> p (j o)"))
             if i >= SCALE_LAG:
                 scale_and_store(i - SCALE_LAG)

from contextlib import ExitStack

import concourse.mybir as mybir
from concourse.masks import make_identity

F32 = mybir.dt.float32
BF16 = mybir.dt.bfloat16
U32 = mybir.dt.uint32
U8 = mybir.dt.uint8
FP8X4 = mybir.dt.float8_e4m3fn_x4
ACT = mybir.ActivationFunctionType
ALU = mybir.AluOpType

P = 128
PACK = 4
BANK = 512

TOKENS = 1024
D_IN = 1024
D_OUT = 1024
RANK = 128
SCALING = 2.0

T_TILES = TOKENS // P
O_TILES = D_OUT // P
PASSES = D_IN // (P * PACK)
HALVES = D_OUT // BANK
O_TILES_PER_HALF = BANK // P
WORD_BLOCKS = D_IN // 2 // P

EARLY = 2
SCALE_LAG = 1
SCALAR_W_BANKS = 2
TILES_MERGED_ON_TENSOR = 3

FLOPS = 2 * TOKENS * D_IN * D_OUT + 2 * TOKENS * RANK * D_OUT + 2 * D_OUT * RANK * D_IN


def merged_on_tensor(j):
    return O_TILES - 1 - TILES_MERGED_ON_TENSOR <= j < O_TILES - 1


def tile_loralinear_pa_kernel(tc, x, weight, a_w, b_w, magnitude, h_lora, out):
    nc = tc.nc
    x_rows = x.flatten_outer_dims().rearrange("(p i) d -> p i d", i=T_TILES)
    h_rows = h_lora.flatten_outer_dims().rearrange("(p i) r -> p i r", i=T_TILES)
    out_rows = out.flatten_outer_dims().rearrange("(p i) o -> p i o", i=T_TILES)

    with ExitStack() as ctx:
        keep = ctx.enter_context(tc.tile_pool(name="keep", bufs=1))
        merged = ctx.enter_context(tc.tile_pool(name="merged", bufs=4))
        psum = ctx.enter_context(tc.psum_pool(name="psum", bufs=7))
        psum_kept = ctx.enter_context(tc.psum_pool(name="psum_kept", bufs=1))
        ctx.enter_context(tc.manual_schedule())

        ident_bf16 = keep.tile([P, P], BF16)
        make_identity(nc, ident_bf16[:])
        ident_f32 = keep.tile([P, P], F32)
        make_identity(nc, ident_f32[:])
        table_warmer = keep.tile([P, 1], F32)
        nc.vector.memset(table_warmer[:], 1.0)
        nc.scalar.sqrt(table_warmer[:], table_warmer[:])
        mag_rows = keep.tile([P, P], BF16)
        nc.vector.memset(mag_rows[:], 0.0)

        b_sb = keep.tile([P, O_TILES, RANK], BF16)
        nc.sync.dma_start(out=b_sb[:], in_=b_w.rearrange("(j p) r -> p j r", p=P))
        a_sb = keep.tile([P, D_IN], BF16)
        nc.sync.dma_start(out=a_sb[:], in_=a_w)
        w_sb = keep.tile([P, O_TILES, D_IN], BF16)
        for j in range(O_TILES):
            nc.sync.dma_start(out=w_sb[:, j, :], in_=weight[j * P : (j + 1) * P, :])
        h_sb = keep.tile([P, T_TILES, RANK], BF16)
        nc.sync.dma_start(out=h_sb[:], in_=h_rows)
        x_sb = keep.tile([P, T_TILES, D_IN], BF16)
        for i in range(0, T_TILES, 2):
            nc.sync.dma_start(out=x_sb[:, i : i + 2, :], in_=x_rows[:, i : i + 2, :])
        nc.sync.dma_start(
            out=mag_rows[0:O_TILES, :], in_=magnitude.rearrange("one (j p) -> (one j) p", p=P)
        )
        w_words = w_sb[:].bitcast(F32)
        x_words = x_sb[:].bitcast(F32)

        b2T = keep.tile([P, D_OUT], BF16)
        hT = keep.tile([P, T_TILES, P], BF16)
        w_grouped = keep.tile([P, HALVES, PASSES, BANK, PACK], BF16, align_bytes=64)
        w_grouped_words = w_grouped[:].bitcast(F32)
        w_codes = keep.tile([P, HALVES, PASSES, BANK], U32, align_bytes=64)
        w_scales = keep.tile([P, HALVES, PASSES, BANK], U8, align_bytes=64)
        x_grouped = keep.tile([P, T_TILES, PASSES, P, PACK], BF16, align_bytes=64)
        x_grouped_words = x_grouped[:].bitcast(F32)
        x_codes = keep.tile([P, T_TILES, PASSES, P], U32, align_bytes=64)
        x_scales = keep.tile([P, T_TILES, PASSES, P], U8, align_bytes=64)
        norm_sq_parts = keep.tile([P, D_IN // BANK, O_TILES], F32)
        nc.vector.memset(norm_sq_parts[:], 0.0)
        m_first = keep.tile([P, BANK], F32)
        m_second = psum_kept.tile([P, O_TILES_PER_HALF, P], F32)
        results = keep.tile([P, T_TILES, D_OUT], F32)

        def turn_words(row_words):
            bank = psum.tile([P, WORD_BLOCKS, P], F32, tag="bank")
            for blk in range(WORD_BLOCKS):
                nc.tensor.transpose(
                    bank[:, blk, :], row_words[:, blk * P : (blk + 1) * P], ident_f32[:]
                )
            return bank

        def group_words(on_vector, grouped_words, bank):
            side_by_side = bank[:].rearrange("p (g u) r -> p g r u", u=2)
            if on_vector:
                nc.vector.tensor_copy(out=grouped_words, in_=side_by_side)
            else:
                nc.scalar.copy(out=grouped_words, in_=side_by_side)

        def group_weight_words(j, bank):
            half, j_in_half = divmod(j, O_TILES_PER_HALF)
            group_words(
                j >= SCALAR_W_BANKS,
                w_grouped_words[:, half, :, j_in_half * P : (j_in_half + 1) * P, :],
                bank,
            )

        def quantise_weight(half):
            nc.vector.quantize_mx(
                out=w_codes[:, half, :, :].rearrange("p g o -> p (g o)").bitcast(FP8X4),
                scales=w_scales[:, half, :, :].rearrange("p g o -> p (g o)"),
                in_=w_grouped[:, half, :, :, :].rearrange("p g o t -> p (g o t)"),
            )

        def quantise_tokens(i):
            nc.vector.quantize_mx(
                out=x_codes[:, i, :, :].rearrange("p g r -> p (g r)").bitcast(FP8X4),
                scales=x_scales[:, i, :, :].rearrange("p g r -> p (g r)"),
                in_=x_grouped[:, i, :, :, :].rearrange("p g r t -> p (g r t)"),
            )

        def adapter_weight_products(j):
            banks = []
            for c in range(D_IN // BANK):
                cols = slice(c * BANK, (c + 1) * BANK)
                ba2 = psum.tile([P, BANK], F32, tag="bank", name="ba2")
                if merged_on_tensor(j):
                    nc.tensor.matmul(
                        out=ba2[:], lhsT=ident_bf16[:], rhs=w_sb[:, j, cols], start=True, stop=False
                    )
                nc.tensor.matmul(
                    out=ba2[:], lhsT=b2T[:, j * P : (j + 1) * P], rhs=a_sb[:, cols],
                    start=(not merged_on_tensor(j)), stop=True,
                )
                banks.append(ba2)
            return banks

        def merge_weight(j, banks, w_eff):
            for c in range(D_IN // BANK):
                cols = slice(c * BANK, (c + 1) * BANK)
                nc.vector.tensor_tensor(
                    out=w_eff[:, cols], in0=banks[c][:], in1=w_sb[:, j, cols], op=ALU.add
                )

        def sum_squares(j, banks, w_eff):
            if merged_on_tensor(j):
                for c in range(D_IN // BANK):
                    nc.scalar.activation(
                        out=w_eff[:, c * BANK : (c + 1) * BANK], in_=banks[c][:], func=ACT.Square,
                        accum_out=norm_sq_parts[:, c, j : j + 1],
                    )
            else:
                nc.scalar.activation(
                    out=w_eff[:], in_=w_eff[:], func=ACT.Square,
                    accum_out=norm_sq_parts[:, 0, j : j + 1],
                )

        def lora_products(i):
            for half in range(HALVES):
                cols = slice(half * BANK, (half + 1) * BANK)
                lora = psum.tile([P, BANK], F32, tag="bank")
                nc.tensor.matmul(
                    out=lora[:], lhsT=hT[:, i, :], rhs=b2T[:, cols], start=True, stop=True
                )
                nc.scalar.copy(out=results[:, i, cols], in_=lora[:])

        def add_base_products(i):
            for half in range(HALVES):
                cols = slice(half * BANK, (half + 1) * BANK)
                base = psum.tile([P, BANK], F32, tag="bank")
                for g in range(PASSES):
                    nc.tensor.matmul_mx(
                        out=base[:],
                        lhsT=x_codes[:, i, g, :].bitcast(FP8X4),
                        lhsT_scale=x_scales[:, i, g, :],
                        rhs=w_codes[:, half, g, :].bitcast(FP8X4),
                        rhs_scale=w_scales[:, half, g, :],
                        start=(g == 0),
                        stop=(g == PASSES - 1),
                    )
                nc.vector.tensor_tensor(
                    out=results[:, i, cols], in0=base[:], in1=results[:, i, cols], op=ALU.add
                )

        def scale_and_store(i):
            nc.gpsimd.tensor_tensor(
                out=results[:, i, 0:BANK], in0=results[:, i, 0:BANK], in1=m_first[:], op=ALU.mult
            )
            nc.sync.dma_start(out=out_rows[:, i, 0:BANK], in_=results[:, i, 0:BANK])
            nc.vector.tensor_tensor(
                out=results[:, i, BANK:D_OUT],
                in0=m_second[:].rearrange("p j o -> p (j o)"),
                in1=results[:, i, BANK:D_OUT],
                op=ALU.mult,
            )
            nc.sync.dma_start(out=out_rows[:, i, BANK:D_OUT], in_=results[:, i, BANK:D_OUT])

        for half in range(HALVES):
            b_turned = psum.tile([P, O_TILES_PER_HALF, P], BF16, tag="bank")
            for j_in_half in range(O_TILES_PER_HALF):
                nc.tensor.transpose(
                    b_turned[:, j_in_half, :],
                    b_sb[:, half * O_TILES_PER_HALF + j_in_half, :],
                    ident_bf16[:],
                )
            nc.scalar.mul(
                out=b2T[:, half * BANK : (half + 1) * BANK],
                in_=b_turned[:].rearrange("r j o -> r (j o)"),
                mul=SCALING,
            )

        for j in range(O_TILES):
            ba2_banks = adapter_weight_products(j)
            w_turned = turn_words(w_words[:, j, :])
            w_eff = merged.tile([P, D_IN], F32)
            if not merged_on_tensor(j):
                merge_weight(j, ba2_banks, w_eff)
            group_weight_words(j, w_turned)
            if j == O_TILES - 1 - EARLY:
                h_turned = psum.tile([P, T_TILES, P], BF16, tag="bank")
                for i in range(T_TILES):
                    nc.tensor.transpose(h_turned[:, i, :], h_sb[:, i, :], ident_bf16[:])
                nc.scalar.copy(out=hT[:], in_=h_turned[:])
            if j >= O_TILES - EARLY:
                i = j - (O_TILES - EARLY)
                group_words(False, x_grouped_words[:, i, :, :, :], turn_words(x_words[:, i, :]))
            sum_squares(j, ba2_banks, w_eff)
            if j == O_TILES_PER_HALF:
                quantise_weight(0)

        mag_turned = psum.tile([P, P], BF16, tag="bank")
        nc.tensor.transpose(mag_turned[:], mag_rows[:], ident_bf16[:])
        mag_col = keep.tile([P, O_TILES], F32)
        nc.vector.tensor_copy(out=mag_col[:], in_=mag_turned[:, 0:O_TILES])

        quantise_tokens(0)
        quantise_weight(1)
        for i in range(1, EARLY):
            quantise_tokens(i)
        norm_sq = keep.tile([P, O_TILES], F32)
        nc.vector.tensor_tensor(
            out=norm_sq[:], in0=norm_sq_parts[:, 0, :], in1=norm_sq_parts[:, 1, :], op=ALU.add
        )
        norm = keep.tile([P, O_TILES], F32)

        for i in range(T_TILES + SCALE_LAG):
            if i < T_TILES:
                lora_products(i)
                if i == 0:
                    nc.scalar.sqrt(norm[:], norm_sq[:])
                if i + EARLY < T_TILES:
                    group_words(
                        False,
                        x_grouped_words[:, i + EARLY, :, :, :],
                        turn_words(x_words[:, i + EARLY, :]),
                    )
                add_base_products(i)
                if i + EARLY < T_TILES:
                    quantise_tokens(i + EARLY)
            if i == 0:
                inv_norm = keep.tile([P, O_TILES], F32)
                nc.vector.reciprocal(out=inv_norm[:], in_=norm[:])
                m_col = keep.tile([P, O_TILES], F32)
                nc.vector.tensor_tensor(out=m_col[:], in0=inv_norm[:], in1=mag_col[:], op=ALU.mult)
            if i == 1:
                m_turned = psum.tile([P, O_TILES_PER_HALF, P], F32, tag="bank")
                for j in range(O_TILES):
                    half, j_in_half = divmod(j, O_TILES_PER_HALF)
                    nc.tensor.transpose(
                        (m_turned, m_second)[half][:, j_in_half, :],
                        m_col[:, j : j + 1].to_broadcast([P, P]),
                        ident_f32[:],
                    )
                nc.scalar.copy(out=m_first[:], in_=m_turned[:].rearrange("p j o -> p (j o)"))
            if i >= SCALE_LAG:
                scale_and_store(i - SCALE_LAG)
